import numpy as np
import ml_dtypes


def mxq(x, axis, fmt="e4m3"):
    dtype, down = {"e4m3": (ml_dtypes.float8_e4m3fn, 7), "e5m2": (ml_dtypes.float8_e5m2, 14)}[fmt]
    v = np.moveaxis(np.asarray(x, np.float32).astype(ml_dtypes.bfloat16).astype(np.float64), axis, -1)
    blocks = v.reshape(v.shape[:-1] + (-1, 32))
    amax = np.abs(blocks).max(-1, keepdims=True)
    byte = np.maximum(np.where(amax > 0, np.frexp(amax)[1] - 1 + 127, 0) - down, 1)
    scale = np.exp2(byte - 127.0)
    codes = (blocks / scale).astype(np.float32).astype(dtype).astype(np.float64)
    return np.moveaxis((codes * scale).reshape(v.shape), -1, axis)


WIDE = False


def mx_kscale(k):
    if not WIDE:
        return np.ones(k)
    levels = np.array([10, -10, 5, -5, 0])
    a = np.random.permutation(np.resize(levels, k // 512 * 4)).reshape(k // 512, 4)
    idx = np.arange(k)
    return np.exp2(a[idx // 512, idx % 128 // 32])


BF16 = ml_dtypes.bfloat16


def bf(x):
    return np.asarray(x, np.float32).astype(BF16)


def f64(x):
    return np.asarray(x).astype(np.float64)


E2M1 = np.array([0.0, 0.5, 1.0, 1.5, 2.0, 3.0, 4.0, 6.0, -0.0, -0.5, -1.0, -1.5, -2.0, -3.0, -4.0, -6.0])


def pack_weight(w, fmt):
    k, n = w.shape
    w = f64(bf(w)).reshape(k // 32, 32, n)
    amax = np.abs(w).max(1)
    if fmt == "e4m3":
        byte = np.frexp(amax)[1] - 1 + 127 - 7
    else:
        mant, ex = np.frexp(amax / 6.0)
        byte = np.where(mant > 0.5, ex, ex - 1) + 127
    byte = np.clip(np.where(amax > 0, byte, 1), 1, 254)
    scaled = (w * np.exp2(127.0 - byte)[:, None, :]).reshape(k, n).astype(np.float32)
    by_word = np.ascontiguousarray(scaled.reshape(k // 512, 128, 4, n).transpose(0, 1, 3, 2))
    if fmt == "e4m3":
        words = by_word.astype(ml_dtypes.float8_e4m3fn).view(np.uint8)
    else:
        c = by_word.astype(ml_dtypes.float4_e2m1fn).view(np.uint8) & 0xF
        words = c[..., 0::2] | (c[..., 1::2] << 4)
    return np.ascontiguousarray(words), np.ascontiguousarray(byte.astype(np.uint8).reshape(k // 512, 16, n))


def unpack_weight(words, scales, fmt):
    g, p, n, _ = words.shape
    if fmt == "e4m3":
        vals = np.ascontiguousarray(words).view(ml_dtypes.float8_e4m3fn).astype(np.float64)
    else:
        nib = np.empty((g, p, n, 4), np.uint8)
        nib[..., 0::2] = words & 0xF
        nib[..., 1::2] = words >> 4
        vals = E2M1[nib]
    vals = vals * np.repeat(np.exp2(scales.astype(np.float64) - 127.0), 8, axis=1)[..., None]
    return vals.transpose(0, 1, 3, 2).reshape(g * 512, n)


B, T, I, H = 128, 4, 16384, 128
FMT = "e4m3"


def sigmoid(v):
    return 1.0 / (1.0 + np.exp(-v))


def setup_inputs():
    s = mx_kscale(I)
    d = {"inputs": bf(np.random.standard_normal((B, T, I)) * s),
         "h0": bf(np.random.standard_normal((1, B, H))),
         "c0": bf(np.random.standard_normal((1, B, H)))}
    for ni, nh in (("ii", "hi"), ("if_", "hf"), ("io", "ho"), ("ig", "hg")):
        w = np.random.standard_normal((H, I)) / np.sqrt(I) / s[None, :]
        words, scales = pack_weight(np.ascontiguousarray(w.T), FMT)
        d["w_" + ni + "_words"] = words
        d["w_" + ni + "_scales"] = scales
        d["b_" + ni] = bf(np.random.standard_normal((H, 1)) * 0.3)
        d["w_" + nh] = bf(np.random.standard_normal((H, H)) * 0.7 / np.sqrt(H))
        d["b_" + nh] = bf(np.random.standard_normal((H, 1)) * 0.3)
    return d


def reference(inputs, h0, c0, w_ii_words, w_ii_scales, b_ii, w_hi, b_hi, w_if__words, w_if__scales, b_if_, w_hf, b_hf, w_io_words, w_io_scales, b_io, w_ho, b_ho, w_ig_words, w_ig_scales, b_ig, w_hg, b_hg):
    xq = mxq(f64(inputs), 2, "e4m3")
    h0s = f64(h0)[0]
    c0s = f64(c0)[0]
    zi = (xq @ unpack_weight(w_ii_words, w_ii_scales, FMT)) + (h0s @ f64(w_hi).T)[:, None, :] + f64(b_ii)[:, 0] + f64(b_hi)[:, 0]
    zf = (xq @ unpack_weight(w_if__words, w_if__scales, FMT)) + (h0s @ f64(w_hf).T)[:, None, :] + f64(b_if_)[:, 0] + f64(b_hf)[:, 0]
    zg = (xq @ unpack_weight(w_ig_words, w_ig_scales, FMT)) + (h0s @ f64(w_hg).T)[:, None, :] + f64(b_ig)[:, 0] + f64(b_hg)[:, 0]
    zo = (xq @ unpack_weight(w_io_words, w_io_scales, FMT)) + (h0s @ f64(w_ho).T)[:, None, :] + f64(b_io)[:, 0] + f64(b_ho)[:, 0]
    i = sigmoid(zi)
    f = sigmoid(zf)
    g = np.tanh(zg)
    o = sigmoid(zo)
    c_next = f * c0s[:, None, :] + i * g
    h_next = o * np.tanh(c_next)
    hidden_seq = np.transpose(h_next, (1, 0, 2))
    h_last = hidden_seq[-1][None]
    c_last = c_next[:, -1][None]
    return hidden_seq, h_last, c_last

@@ -1,0 +1,216 @@
+from contextlib import ExitStack
+
+import concourse.mybir as mybir
+from concourse.masks import make_identity
+
+BF16 = mybir.dt.bfloat16
+F32 = mybir.dt.float32
+I32 = mybir.dt.int32
+U32 = mybir.dt.uint32
+U8 = mybir.dt.uint8
+FP8X4 = mybir.dt.float8_e4m3fn_x4
+ACT = mybir.ActivationFunctionType
+ALU = mybir.AluOpType
+
+P = 128
+B, T, I, H = 128, 4, 16384, 128
+GATES = 4
+K_PASS = 512
+GROUPS = I // K_PASS
+ROUND_GROUPS = 2
+ROUNDS = GROUPS // ROUND_GROUPS
+ROUND_K = ROUND_GROUPS * K_PASS
+W_LOAD_GROUPS = 4
+HIDDEN_ROUND = ROUNDS // 2
+
+FLOPS = 2 * B * T * I * GATES * H + 2 * B * H * GATES * H
+
+
+def tile_naivelstm_pa_k_kernel(
+    tc,
+    inputs, h0, c0,
+    w_ii_words, w_ii_scales, b_ii, w_hi, b_hi,
+    w_if__words, w_if__scales, b_if_, w_hf, b_hf,
+    w_io_words, w_io_scales, b_io, w_ho, b_ho,
+    w_ig_words, w_ig_scales, b_ig, w_hg, b_hg,
+    out_0, out_1, out_2,
+):
+    nc = tc.nc
+    gate_words = [w_ii_words, w_if__words, w_io_words, w_ig_words]
+    gate_scales = [w_ii_scales, w_if__scales, w_io_scales, w_ig_scales]
+    gate_bias_x = [b_ii, b_if_, b_io, b_ig]
+    gate_bias_h = [b_hi, b_hf, b_ho, b_hg]
+    gate_w_h = [w_hi, w_hf, w_ho, w_hg]
+
+    with ExitStack() as ctx:
+        keep = ctx.enter_context(tc.tile_pool(name="keep", bufs=1))
+        x_pool = ctx.enter_context(tc.tile_pool(name="x_pool", bufs=6))
+        q_pool = ctx.enter_context(tc.tile_pool(name="q_pool", bufs=3))
+        work = ctx.enter_context(tc.tile_pool(name="work", bufs=T))
+        acc_pool = ctx.enter_context(tc.psum_pool(name="acc_pool", bufs=1))
+        xt_pool = ctx.enter_context(tc.psum_pool(name="xt_pool", bufs=4))
+        ctx.enter_context(tc.manual_schedule())
+
+        warm = keep.tile([P, 1], F32)
+        nc.vector.memset(warm[:], 0.0)
+        nc.scalar.activation(out=warm[:], in_=warm[:], func=ACT.Sigmoid)
+
+        w_planes = keep.tile([P, GROUPS, GATES * H], U8, align_bytes=64)
+        nc.vector.memset(w_planes[:].rearrange("p g n -> p (g n)").bitcast(I32), 0)
+        w_codes = keep.tile([P, GROUPS, GATES * H], U32, align_bytes=64)
+
+        ident_f32 = keep.tile([P, P], F32)
+        make_identity(nc, ident_f32[:])
+        ident_bf16 = keep.tile([P, P], BF16)
+        make_identity(nc, ident_bf16[:])
+        ones = keep.tile([P, P], BF16)
+        nc.vector.memset(ones[:], 1.0)
+        bias_rows = keep.tile([P, GATES * H], BF16)
+        nc.vector.memset(bias_rows[:], 0.0)
+
+        rec_rows = keep.tile([P, 1 + GATES, H], BF16)
+        nc.gpsimd.dma_start(out=rec_rows[:, 0, :], in_=h0[0])
+        for j in range(GATES):
+            nc.gpsimd.dma_start(out=rec_rows[:, 1 + j, :], in_=gate_w_h[j])
+        for j in range(GATES):
+            cols = slice(j * H, (j + 1) * H)
+            nc.gpsimd.dma_start(out=bias_rows[0:1, cols], in_=gate_bias_x[j].rearrange("h o -> o h"))
+            nc.gpsimd.dma_start(out=bias_rows[1:2, cols], in_=gate_bias_h[j].rearrange("h o -> o h"))
+        c0_sb = keep.tile([P, H], BF16)
+        nc.gpsimd.dma_start(out=c0_sb[:], in_=c0[0])
+
+        def load_x(r):
+            x_raw = x_pool.tile([P, T, ROUND_K], BF16, name="x_raw")
+            nc.sync.dma_start(out=x_raw[:], in_=inputs[:, :, r * ROUND_K : (r + 1) * ROUND_K])
+            return x_raw
+
+        def load_scales():
+            for j in range(GATES):
+                rows = gate_scales[j].rearrange("g (q r) n -> r q g n", r=4)
+                for r in range(4):
+                    nc.sync.dma_start(
+                        out=w_planes[r : P : 32, :, j * H : (j + 1) * H].bitcast(I32),
+                        in_=rows[r].bitcast(I32),
+                    )
+
+        def load_weights(first_group):
+            groups = slice(first_group, first_group + W_LOAD_GROUPS)
+            for j in range(GATES):
+                words = gate_words[j].rearrange("g p n t -> p g (n t)")
+                nc.sync.dma_start(
+                    out=w_codes[:, groups, j * H : (j + 1) * H].bitcast(I32),
+                    in_=words[:, groups, :].bitcast(I32),
+                )
+
+        x_tiles = []
+        for r in range(ROUNDS):
+            x_tiles.append(load_x(r))
+            if r == 0:
+                load_scales()
+            if (r * ROUND_GROUPS) % W_LOAD_GROUPS == 0:
+                load_weights(r * ROUND_GROUPS)
+
+        acc = [acc_pool.tile([P, GATES * H], F32, name="acc%d" % t) for t in range(T)]
+        x_quantised = {}
+
+        def transpose_round(r):
+            x_raw = x_tiles[r]
+            grouped = q_pool.tile([P, ROUND_GROUPS, 2, 2 * B, 4], BF16, name="grouped", align_bytes=64)
+            x_codes = q_pool.tile([P, ROUND_GROUPS, T * B], U32, name="x_codes", align_bytes=64)
+            x_planes = q_pool.tile([P, ROUND_GROUPS, T * B], U8, name="x_planes", align_bytes=64)
+            for gl in range(ROUND_GROUPS):
+                for half in range(2):
+                    xt = xt_pool.tile([P, 2, 2 * B], F32, name="xt")
+                    for tl in range(2):
+                        x_words = x_raw[:, 2 * half + tl, :].bitcast(F32)
+                        for u in range(2):
+                            nc.tensor.transpose(
+                                xt[:, u, tl * B : (tl + 1) * B],
+                                x_words[:, 256 * gl + u : 256 * (gl + 1) : 2],
+                                ident_f32[:],
+                            )
+                    copy = nc.scalar.copy if half == 0 else nc.vector.tensor_copy
+                    copy(out=grouped[:, gl, half].bitcast(F32), in_=xt[:].rearrange("p u c -> p c u"))
+            for gl in range(ROUND_GROUPS):
+                nc.vector.quantize_mx(
+                    out=x_codes[:, gl, :].bitcast(FP8X4),
+                    scales=x_planes[:, gl, :],
+                    in_=grouped[:, gl].rearrange("p h c j -> p (h c j)"),
+                )
+            x_quantised[r] = (x_codes, x_planes)
+
+        def multiply_round(r):
+            x_codes, x_planes = x_quantised[r]
+            for gl in range(ROUND_GROUPS):
+                g = r * ROUND_GROUPS + gl
+                for t in range(T):
+                    rows = slice(t * B, (t + 1) * B)
+                    nc.tensor.matmul_mx(
+                        out=acc[t][:],
+                        lhsT=x_codes[:, gl, rows].bitcast(FP8X4),
+                        lhsT_scale=x_planes[:, gl, rows],
+                        rhs=w_codes[:, g, :].bitcast(FP8X4),
+                        rhs_scale=w_planes[:, g, :],
+                        start=(g == 0),
+                        stop=(g == GROUPS - 1),
+                    )
+
+        rec_cols = keep.tile([P, 1 + GATES, H], BF16)
+        hidden = keep.tile([P, GATES * H], F32)
+
+        def transpose_recurrent():
+            rec_ps = xt_pool.tile([P, 1 + GATES, H], BF16, name="rec_ps", tag="xt")
+            for j in range(1 + GATES):
+                nc.tensor.transpose(rec_ps[:, j, :], rec_rows[:, j, :], ident_bf16[:])
+            nc.scalar.copy(out=rec_cols[:], in_=rec_ps[:])
+
+        def multiply_recurrent():
+            hid_ps = xt_pool.tile([P, GATES * H], F32, name="hid_ps", tag="xt")
+            nc.tensor.matmul(
+                out=hid_ps[:],
+                lhsT=rec_cols[:, 0, :],
+                rhs=rec_cols[:, 1:, :].rearrange("p j n -> p (j n)"),
+                start=True,
+                stop=False,
+            )
+            nc.tensor.matmul(out=hid_ps[:], lhsT=ones[:], rhs=bias_rows[:], start=False, stop=True)
+            nc.scalar.copy(out=hidden[:], in_=hid_ps[:])
+
+        transpose_round(0)
+        for r in range(1, ROUNDS):
+            transpose_round(r)
+            if r == HIDDEN_ROUND:
+                transpose_recurrent()
+            if r == HIDDEN_ROUND + 1:
+                multiply_recurrent()
+            multiply_round(r - 1)
+        multiply_round(ROUNDS - 1)
+
+        gates = []
+        for t in range(T):
+            z = work.tile([P, GATES * H], F32, name="z")
+            nc.vector.tensor_tensor(out=z[:], in0=acc[t][:], in1=hidden[:], op=ALU.add)
+            gate = work.tile([P, GATES, H], F32, name="gate")
+            flat = gate[:].rearrange("p j n -> p (j n)")
+            nc.scalar.activation(out=flat[:, 0 : 3 * H], in_=z[:, 0 : 3 * H], func=ACT.Sigmoid)
+            nc.scalar.activation(out=flat[:, 3 * H :], in_=z[:, 3 * H :], func=ACT.Tanh)
+            gates.append(gate)
+        cells = []
+        for t in range(T):
+            gate = gates[t]
+            kept = work.tile([P, H], F32, name="kept")
+            nc.vector.tensor_tensor(out=kept[:], in0=gate[:, 1, :], in1=c0_sb[:], op=ALU.mult)
+            fresh = work.tile([P, H], F32, name="fresh")
+            nc.vector.tensor_tensor(out=fresh[:], in0=gate[:, 0, :], in1=gate[:, 3, :], op=ALU.mult)
+            c_next = work.tile([P, H], F32, name="c_next")
+            nc.vector.tensor_tensor(out=c_next[:], in0=kept[:], in1=fresh[:], op=ALU.add)
+            tanh_c = work.tile([P, H], F32, name="tanh_c")
+            nc.scalar.activation(out=tanh_c[:], in_=c_next[:], func=ACT.Tanh)
+            cells.append((c_next, tanh_c))
+        nc.sync.dma_start(out=out_2[0], in_=cells[T - 1][0][:])
+        for t in range(T):
+            h_next = work.tile([P, H], F32, name="h_next")
+            nc.vector.tensor_tensor(out=h_next[:], in0=gates[t][:, 2, :], in1=cells[t][1][:], op=ALU.mult)
+            nc.sync.dma_start(out=out_0[t], in_=h_next[:])
+            if t == T - 1:
+                nc.sync.dma_start(out=out_1[0], in_=h_next[:])

@@ -17,11 +17,14 @@ B, T, I, H = 128, 4, 16384, 128
 GATES = 4
 K_PASS = 512
 GROUPS = I // K_PASS
-ROUND_GROUPS = 2
-ROUNDS = GROUPS // ROUND_GROUPS
-ROUND_K = ROUND_GROUPS * K_PASS
+CHUNK_GROUPS = 8
+CHUNK_K = CHUNK_GROUPS * K_PASS
+CHUNKS = GROUPS // CHUNK_GROUPS
+X_RUNS = CHUNKS * T
+MX_RUN_GROUPS = 2
+MX_RUNS = GROUPS // MX_RUN_GROUPS
+LEAD = T
 W_LOAD_GROUPS = 4
-HIDDEN_ROUND = ROUNDS // 2
 
 FLOPS = 2 * B * T * I * GATES * H + 2 * B * H * GATES * H
 
@@ -44,8 +47,8 @@ def tile_naivelstm_pa_k_kernel(
 
     with ExitStack() as ctx:
         keep = ctx.enter_context(tc.tile_pool(name="keep", bufs=1))
-        x_pool = ctx.enter_context(tc.tile_pool(name="x_pool", bufs=6))
-        q_pool = ctx.enter_context(tc.tile_pool(name="q_pool", bufs=3))
+        x_pool = ctx.enter_context(tc.tile_pool(name="x_pool", bufs=4))
+        stage = ctx.enter_context(tc.tile_pool(name="stage", bufs=2))
         work = ctx.enter_context(tc.tile_pool(name="work", bufs=T))
         acc_pool = ctx.enter_context(tc.psum_pool(name="acc_pool", bufs=1))
         xt_pool = ctx.enter_context(tc.psum_pool(name="xt_pool", bufs=4))
@@ -55,12 +58,20 @@ def tile_naivelstm_pa_k_kernel(
         nc.vector.memset(warm[:], 0.0)
         nc.scalar.activation(out=warm[:], in_=warm[:], func=ACT.Sigmoid)
 
-        w_planes = keep.tile([P, GROUPS, GATES * H], U8, align_bytes=64)
-        nc.vector.memset(w_planes[:].rearrange("p g n -> p (g n)").bitcast(I32), 0)
-        w_codes = keep.tile([P, GROUPS, GATES * H], U32, align_bytes=64)
-
         ident_f32 = keep.tile([P, P], F32)
         make_identity(nc, ident_f32[:])
+
+        w_planes = keep.tile([P, GROUPS, GATES * H], U8, align_bytes=64)
+        for j in range(GATES):
+            nc.vector.memset(w_planes[:, :, j * H : (j + 1) * H].bitcast(I32), 0)
+        for j in range(GATES):
+            scale_rows = gate_scales[j].rearrange("g (q r) n -> r q g n", r=4)
+            for r in range(4):
+                nc.gpsimd.dma_start(
+                    out=w_planes[r : P : 32, :, j * H : (j + 1) * H].bitcast(F32),
+                    in_=scale_rows[r].bitcast(F32),
+                )
+
         ident_bf16 = keep.tile([P, P], BF16)
         make_identity(nc, ident_bf16[:])
         ones = keep.tile([P, P], BF16)
@@ -79,19 +90,13 @@ def tile_naivelstm_pa_k_kernel(
         c0_sb = keep.tile([P, H], BF16)
         nc.gpsimd.dma_start(out=c0_sb[:], in_=c0[0])
 
-        def load_x(r):
-            x_raw = x_pool.tile([P, T, ROUND_K], BF16, name="x_raw")
-            nc.sync.dma_start(out=x_raw[:], in_=inputs[:, :, r * ROUND_K : (r + 1) * ROUND_K])
-            return x_raw
+        w_codes = keep.tile([P, GROUPS, GATES * H], U32, align_bytes=64)
 
-        def load_scales():
-            for j in range(GATES):
-                rows = gate_scales[j].rearrange("g (q r) n -> r q g n", r=4)
-                for r in range(4):
-                    nc.sync.dma_start(
-                        out=w_planes[r : P : 32, :, j * H : (j + 1) * H].bitcast(I32),
-                        in_=rows[r].bitcast(I32),
-                    )
+        def load_x(n):
+            chunk, t = divmod(n, T)
+            x_raw = x_pool.tile([P, CHUNK_K], BF16, name="x_raw")
+            nc.sync.dma_start(out=x_raw[:], in_=inputs[:, t, chunk * CHUNK_K : (chunk + 1) * CHUNK_K])
+            return x_raw
 
         def load_weights(first_group):
             groups = slice(first_group, first_group + W_LOAD_GROUPS)
@@ -102,53 +107,57 @@ def tile_naivelstm_pa_k_kernel(
                     in_=words[:, groups, :].bitcast(I32),
                 )
 
-        x_tiles = []
-        for r in range(ROUNDS):
-            x_tiles.append(load_x(r))
-            if r == 0:
-                load_scales()
-            if (r * ROUND_GROUPS) % W_LOAD_GROUPS == 0:
-                load_weights(r * ROUND_GROUPS)
+        x_tiles = [load_x(n) for n in range(LEAD)]
+        for m in range(MX_RUNS):
+            if m + LEAD < X_RUNS:
+                x_tiles.append(load_x(m + LEAD))
+            if (m * MX_RUN_GROUPS) % W_LOAD_GROUPS == 0:
+                load_weights(m * MX_RUN_GROUPS)
 
         acc = [acc_pool.tile([P, GATES * H], F32, name="acc%d" % t) for t in range(T)]
-        x_quantised = {}
+        x_sorted = {}
+        x_grouped = {}
+        x_codes = {}
+        x_planes = {}
 
-        def transpose_round(r):
-            x_raw = x_tiles[r]
-            grouped = q_pool.tile([P, ROUND_GROUPS, 2, 2 * B, 4], BF16, name="grouped", align_bytes=64)
-            x_codes = q_pool.tile([P, ROUND_GROUPS, T * B], U32, name="x_codes", align_bytes=64)
-            x_planes = q_pool.tile([P, ROUND_GROUPS, T * B], U8, name="x_planes", align_bytes=64)
-            for gl in range(ROUND_GROUPS):
-                for half in range(2):
-                    xt = xt_pool.tile([P, 2, 2 * B], F32, name="xt")
-                    for tl in range(2):
-                        x_words = x_raw[:, 2 * half + tl, :].bitcast(F32)
-                        for u in range(2):
-                            nc.tensor.transpose(
-                                xt[:, u, tl * B : (tl + 1) * B],
-                                x_words[:, 256 * gl + u : 256 * (gl + 1) : 2],
-                                ident_f32[:],
-                            )
-                    copy = nc.scalar.copy if half == 0 else nc.vector.tensor_copy
-                    copy(out=grouped[:, gl, half].bitcast(F32), in_=xt[:].rearrange("p u c -> p c u"))
-            for gl in range(ROUND_GROUPS):
-                nc.vector.quantize_mx(
-                    out=x_codes[:, gl, :].bitcast(FP8X4),
-                    scales=x_planes[:, gl, :],
-                    in_=grouped[:, gl].rearrange("p h c j -> p (h c j)"),
+        def sort_x(n):
+            x_sorted[n] = stage.tile([P, CHUNK_GROUPS, 2, P], F32, name="x_sorted")
+            nc.vector.tensor_copy(
+                out=x_sorted[n][:],
+                in_=x_tiles[n][:].bitcast(F32).rearrange("b (g p u) -> b g u p", p=P, u=2),
+            )
+
+        def transpose_x(n):
+            x_grouped[n] = stage.tile([P, CHUNK_GROUPS, B, 4], BF16, name="x_grouped", align_bytes=64)
+            for first in range(0, CHUNK_GROUPS, 2):
+                xt = xt_pool.tile([P, 2, 2, B], F32, name="xt")
+                for gl in range(2):
+                    for u in range(2):
+                        nc.tensor.transpose(xt[:, gl, u, :], x_sorted[n][:, first + gl, u, :], ident_f32[:])
+                nc.scalar.copy(
+                    out=x_grouped[n][:, first : first + 2].bitcast(F32),
+                    in_=xt[:].rearrange("p g u b -> p g b u"),
                 )
-            x_quantised[r] = (x_codes, x_planes)
 
-        def multiply_round(r):
-            x_codes, x_planes = x_quantised[r]
-            for gl in range(ROUND_GROUPS):
-                g = r * ROUND_GROUPS + gl
-                for t in range(T):
-                    rows = slice(t * B, (t + 1) * B)
+        def quantise_x(n):
+            chunk, t = divmod(n, T)
+            if t == 0:
+                x_codes[chunk] = stage.tile([P, T, CHUNK_GROUPS, B], U32, name="x_codes", align_bytes=64)
+                x_planes[chunk] = stage.tile([P, T, CHUNK_GROUPS, B], U8, name="x_planes", align_bytes=64)
+            nc.vector.quantize_mx(
+                out=x_codes[chunk][:, t].rearrange("p g b -> p (g b)").bitcast(FP8X4),
+                scales=x_planes[chunk][:, t].rearrange("p g b -> p (g b)"),
+                in_=x_grouped[n][:].rearrange("p g b j -> p (g b j)"),
+            )
+
+        def multiply_run(m):
+            for t in range(T):
+                for g in range(m * MX_RUN_GROUPS, (m + 1) * MX_RUN_GROUPS):
+                    chunk, gl = divmod(g, CHUNK_GROUPS)
                     nc.tensor.matmul_mx(
                         out=acc[t][:],
-                        lhsT=x_codes[:, gl, rows].bitcast(FP8X4),
-                        lhsT_scale=x_planes[:, gl, rows],
+                        lhsT=x_codes[chunk][:, t, gl, :].bitcast(FP8X4),
+                        lhsT_scale=x_planes[chunk][:, t, gl, :],
                         rhs=w_codes[:, g, :].bitcast(FP8X4),
                         rhs_scale=w_planes[:, g, :],
                         start=(g == 0),
@@ -176,15 +185,19 @@ def tile_naivelstm_pa_k_kernel(
             nc.tensor.matmul(out=hid_ps[:], lhsT=ones[:], rhs=bias_rows[:], start=False, stop=True)
             nc.scalar.copy(out=hidden[:], in_=hid_ps[:])
 
-        transpose_round(0)
-        for r in range(1, ROUNDS):
-            transpose_round(r)
-            if r == HIDDEN_ROUND:
-                transpose_recurrent()
-            if r == HIDDEN_ROUND + 1:
-                multiply_recurrent()
-            multiply_round(r - 1)
-        multiply_round(ROUNDS - 1)
+        sort_x(0)
+        for n in range(X_RUNS):
+            if n + 1 < X_RUNS:
+                sort_x(n + 1)
+            transpose_x(n)
+            quantise_x(n)
+            if n >= LEAD:
+                multiply_run(n - LEAD)
+        transpose_recurrent()
+        multiply_run(X_RUNS - LEAD)
+        multiply_recurrent()
+        for m in range(X_RUNS - LEAD + 1, MX_RUNS):
+            multiply_run(m)
 
         gates = []
         for t in range(T):

@@ -64,13 +64,6 @@ def tile_naivelstm_pa_k_kernel(
         w_planes = keep.tile([P, GROUPS, GATES * H], U8, align_bytes=64)
         for j in range(GATES):
             nc.vector.memset(w_planes[:, :, j * H : (j + 1) * H].bitcast(I32), 0)
-        for j in range(GATES):
-            scale_rows = gate_scales[j].rearrange("g (q r) n -> r q g n", r=4)
-            for r in range(4):
-                nc.gpsimd.dma_start(
-                    out=w_planes[r : P : 32, :, j * H : (j + 1) * H].bitcast(F32),
-                    in_=scale_rows[r].bitcast(F32),
-                )
 
         ident_bf16 = keep.tile([P, P], BF16)
         make_identity(nc, ident_bf16[:])
@@ -107,7 +100,18 @@ def tile_naivelstm_pa_k_kernel(
                     in_=words[:, groups, :].bitcast(I32),
                 )
 
-        x_tiles = [load_x(n) for n in range(LEAD)]
+        def load_scales(j):
+            scale_rows = gate_scales[j].rearrange("g (q r) n -> r q g n", r=4)
+            for r in range(4):
+                nc.sync.dma_start(
+                    out=w_planes[r : P : 32, :, j * H : (j + 1) * H].bitcast(I32),
+                    in_=scale_rows[r].bitcast(I32),
+                )
+
+        x_tiles = []
+        for n in range(LEAD):
+            x_tiles.append(load_x(n))
+            load_scales(n)
         for m in range(MX_RUNS):
             if m + LEAD < X_RUNS:
                 x_tiles.append(load_x(m + LEAD))

@@ -24,7 +24,7 @@ X_RUNS = CHUNKS * T
 MX_RUN_GROUPS = 2
 MX_RUNS = GROUPS // MX_RUN_GROUPS
 LEAD = T
-W_LOAD_GROUPS = 4
+SYNC_SCALE_GROUPS = 16
 
 FLOPS = 2 * B * T * I * GATES * H + 2 * B * H * GATES * H
 
@@ -65,6 +65,17 @@ def tile_naivelstm_pa_k_kernel(
         for j in range(GATES):
             nc.vector.memset(w_planes[:, :, j * H : (j + 1) * H].bitcast(I32), 0)
 
+        def load_scales(queue, view, j, groups):
+            scale_rows = gate_scales[j].rearrange("g (q r) n -> r q g n", r=4)
+            for r in range(4):
+                queue.dma_start(
+                    out=w_planes[r : P : 32, groups, j * H : (j + 1) * H].bitcast(view),
+                    in_=scale_rows[r][:, groups, :].bitcast(view),
+                )
+
+        for j in range(GATES):
+            load_scales(nc.gpsimd, F32, j, slice(SYNC_SCALE_GROUPS, GROUPS))
+
         ident_bf16 = keep.tile([P, P], BF16)
         make_identity(nc, ident_bf16[:])
         ones = keep.tile([P, P], BF16)
@@ -91,8 +102,8 @@ def tile_naivelstm_pa_k_kernel(
             nc.sync.dma_start(out=x_raw[:], in_=inputs[:, t, chunk * CHUNK_K : (chunk + 1) * CHUNK_K])
             return x_raw
 
-        def load_weights(first_group):
-            groups = slice(first_group, first_group + W_LOAD_GROUPS)
+        def load_weights(m):
+            groups = slice(m * MX_RUN_GROUPS, (m + 1) * MX_RUN_GROUPS)
             for j in range(GATES):
                 words = gate_words[j].rearrange("g p n t -> p g (n t)")
                 nc.sync.dma_start(
@@ -100,23 +111,14 @@ def tile_naivelstm_pa_k_kernel(
                     in_=words[:, groups, :].bitcast(I32),
                 )
 
-        def load_scales(j):
-            scale_rows = gate_scales[j].rearrange("g (q r) n -> r q g n", r=4)
-            for r in range(4):
-                nc.sync.dma_start(
-                    out=w_planes[r : P : 32, :, j * H : (j + 1) * H].bitcast(I32),
-                    in_=scale_rows[r].bitcast(I32),
-                )
-
         x_tiles = []
         for n in range(LEAD):
             x_tiles.append(load_x(n))
-            load_scales(n)
+            load_scales(nc.sync, I32, n, slice(0, SYNC_SCALE_GROUPS))
         for m in range(MX_RUNS):
             if m + LEAD < X_RUNS:
                 x_tiles.append(load_x(m + LEAD))
-            if (m * MX_RUN_GROUPS) % W_LOAD_GROUPS == 0:
-                load_weights(m * MX_RUN_GROUPS)
+            load_weights(m)
 
         acc = [acc_pool.tile([P, GATES * H], F32, name="acc%d" % t) for t in range(T)]
         x_sorted = {}

@@ -17,13 +17,11 @@ B, T, I, H = 128, 4, 16384, 128
 GATES = 4
 K_PASS = 512
 GROUPS = I // K_PASS
-CHUNK_GROUPS = 8
-CHUNK_K = CHUNK_GROUPS * K_PASS
-CHUNKS = GROUPS // CHUNK_GROUPS
-X_RUNS = CHUNKS * T
-MX_RUN_GROUPS = 2
-MX_RUNS = GROUPS // MX_RUN_GROUPS
-LEAD = T
+UNIT_GROUPS = 2
+UNIT_K = UNIT_GROUPS * K_PASS
+UNITS = GROUPS // UNIT_GROUPS
+SLOTS = T * UNIT_GROUPS
+RECURRENT_AT = UNITS // 2
 SYNC_SCALE_GROUPS = 16
 
 FLOPS = 2 * B * T * I * GATES * H + 2 * B * H * GATES * H
@@ -47,8 +45,9 @@ def tile_naivelstm_pa_k_kernel(
 
     with ExitStack() as ctx:
         keep = ctx.enter_context(tc.tile_pool(name="keep", bufs=1))
-        x_pool = ctx.enter_context(tc.tile_pool(name="x_pool", bufs=4))
+        x_pool = ctx.enter_context(tc.tile_pool(name="x_pool", bufs=6))
         stage = ctx.enter_context(tc.tile_pool(name="stage", bufs=2))
+        coded = ctx.enter_context(tc.tile_pool(name="coded", bufs=3))
         work = ctx.enter_context(tc.tile_pool(name="work", bufs=T))
         acc_pool = ctx.enter_context(tc.psum_pool(name="acc_pool", bufs=1))
         xt_pool = ctx.enter_context(tc.psum_pool(name="xt_pool", bufs=4))
@@ -97,13 +96,12 @@ def tile_naivelstm_pa_k_kernel(
         w_codes = keep.tile([P, GROUPS, GATES * H], U32, align_bytes=64)
 
         def load_x(n):
-            chunk, t = divmod(n, T)
-            x_raw = x_pool.tile([P, CHUNK_K], BF16, name="x_raw")
-            nc.sync.dma_start(out=x_raw[:], in_=inputs[:, t, chunk * CHUNK_K : (chunk + 1) * CHUNK_K])
+            x_raw = x_pool.tile([P, T, UNIT_K], BF16, name="x_raw")
+            nc.sync.dma_start(out=x_raw[:], in_=inputs[:, :, n * UNIT_K : (n + 1) * UNIT_K])
             return x_raw
 
         def load_weights(m):
-            groups = slice(m * MX_RUN_GROUPS, (m + 1) * MX_RUN_GROUPS)
+            groups = slice(m * UNIT_GROUPS, (m + 1) * UNIT_GROUPS)
             for j in range(GATES):
                 words = gate_words[j].rearrange("g p n t -> p g (n t)")
                 nc.sync.dma_start(
@@ -111,14 +109,13 @@ def tile_naivelstm_pa_k_kernel(
                     in_=words[:, groups, :].bitcast(I32),
                 )
 
-        x_tiles = []
-        for n in range(LEAD):
-            x_tiles.append(load_x(n))
-            load_scales(nc.sync, I32, n, slice(0, SYNC_SCALE_GROUPS))
-        for m in range(MX_RUNS):
-            if m + LEAD < X_RUNS:
-                x_tiles.append(load_x(m + LEAD))
+        x_tiles = [load_x(0), load_x(1)]
+        for j in range(GATES):
+            load_scales(nc.sync, I32, j, slice(0, SYNC_SCALE_GROUPS))
+        for m in range(UNITS):
             load_weights(m)
+            if m + 2 < UNITS:
+                x_tiles.append(load_x(m + 2))
 
         acc = [acc_pool.tile([P, GATES * H], F32, name="acc%d" % t) for t in range(T)]
         x_sorted = {}
@@ -127,15 +124,15 @@ def tile_naivelstm_pa_k_kernel(
         x_planes = {}
 
         def sort_x(n):
-            x_sorted[n] = stage.tile([P, CHUNK_GROUPS, 2, P], F32, name="x_sorted")
+            x_sorted[n] = stage.tile([P, SLOTS, 2, P], F32, name="x_sorted")
             nc.vector.tensor_copy(
                 out=x_sorted[n][:],
-                in_=x_tiles[n][:].bitcast(F32).rearrange("b (g p u) -> b g u p", p=P, u=2),
+                in_=x_tiles[n][:].rearrange("b t k -> b (t k)").bitcast(F32).rearrange("b (s p u) -> b s u p", p=P, u=2),
             )
 
         def transpose_x(n):
-            x_grouped[n] = stage.tile([P, CHUNK_GROUPS, B, 4], BF16, name="x_grouped", align_bytes=64)
-            for first in range(0, CHUNK_GROUPS, 2):
+            x_grouped[n] = stage.tile([P, SLOTS, B, 4], BF16, name="x_grouped", align_bytes=64)
+            for first in range(0, SLOTS, 2):
                 xt = xt_pool.tile([P, 2, 2, B], F32, name="xt")
                 for gl in range(2):
                     for u in range(2):
@@ -146,24 +143,22 @@ def tile_naivelstm_pa_k_kernel(
                 )
 
         def quantise_x(n):
-            chunk, t = divmod(n, T)
-            if t == 0:
-                x_codes[chunk] = stage.tile([P, T, CHUNK_GROUPS, B], U32, name="x_codes", align_bytes=64)
-                x_planes[chunk] = stage.tile([P, T, CHUNK_GROUPS, B], U8, name="x_planes", align_bytes=64)
+            x_codes[n] = coded.tile([P, SLOTS, B], U32, name="x_codes", align_bytes=64)
+            x_planes[n] = coded.tile([P, SLOTS, B], U8, name="x_planes", align_bytes=64)
             nc.vector.quantize_mx(
-                out=x_codes[chunk][:, t].rearrange("p g b -> p (g b)").bitcast(FP8X4),
-                scales=x_planes[chunk][:, t].rearrange("p g b -> p (g b)"),
-                in_=x_grouped[n][:].rearrange("p g b j -> p (g b j)"),
+                out=x_codes[n][:].rearrange("p s b -> p (s b)").bitcast(FP8X4),
+                scales=x_planes[n][:].rearrange("p s b -> p (s b)"),
+                in_=x_grouped[n][:].rearrange("p s b j -> p (s b j)"),
             )
 
         def multiply_run(m):
             for t in range(T):
-                for g in range(m * MX_RUN_GROUPS, (m + 1) * MX_RUN_GROUPS):
-                    chunk, gl = divmod(g, CHUNK_GROUPS)
+                for gl in range(UNIT_GROUPS):
+                    g = m * UNIT_GROUPS + gl
                     nc.tensor.matmul_mx(
                         out=acc[t][:],
-                        lhsT=x_codes[chunk][:, t, gl, :].bitcast(FP8X4),
-                        lhsT_scale=x_planes[chunk][:, t, gl, :],
+                        lhsT=x_codes[m][:, t * UNIT_GROUPS + gl, :].bitcast(FP8X4),
+                        lhsT_scale=x_planes[m][:, t * UNIT_GROUPS + gl, :],
                         rhs=w_codes[:, g, :].bitcast(FP8X4),
                         rhs_scale=w_planes[:, g, :],
                         start=(g == 0),
@@ -192,18 +187,18 @@ def tile_naivelstm_pa_k_kernel(
             nc.scalar.copy(out=hidden[:], in_=hid_ps[:])
 
         sort_x(0)
-        for n in range(X_RUNS):
-            if n + 1 < X_RUNS:
+        transpose_x(0)
+        for n in range(UNITS):
+            if n + 1 < UNITS:
                 sort_x(n + 1)
-            transpose_x(n)
             quantise_x(n)
-            if n >= LEAD:
-                multiply_run(n - LEAD)
-        transpose_recurrent()
-        multiply_run(X_RUNS - LEAD)
-        multiply_recurrent()
-        for m in range(X_RUNS - LEAD + 1, MX_RUNS):
-            multiply_run(m)
+            if n + 1 < UNITS:
+                transpose_x(n + 1)
+            if n == RECURRENT_AT:
+                transpose_recurrent()
+            multiply_run(n)
+            if n == RECURRENT_AT:
+                multiply_recurrent()
 
         gates = []
         for t in range(T):

@@ -21,7 +21,7 @@ UNIT_GROUPS = 2
 UNIT_K = UNIT_GROUPS * K_PASS
 UNITS = GROUPS // UNIT_GROUPS
 SLOTS = T * UNIT_GROUPS
-RECURRENT_AT = UNITS // 2
+RECURRENT_AT = UNITS - 2
 SYNC_SCALE_GROUPS = 16
 
 FLOPS = 2 * B * T * I * GATES * H + 2 * B * H * GATES * H

@@ -22,7 +22,7 @@ UNIT_K = UNIT_GROUPS * K_PASS
 UNITS = GROUPS // UNIT_GROUPS
 SLOTS = T * UNIT_GROUPS
 RECURRENT_AT = UNITS - 2
-SYNC_SCALE_GROUPS = 16
+SYNC_SCALE_GROUPS = 32
 
 FLOPS = 2 * B * T * I * GATES * H + 2 * B * H * GATES * H
 
@@ -72,8 +72,9 @@ def tile_naivelstm_pa_k_kernel(
                     in_=scale_rows[r][:, groups, :].bitcast(view),
                 )
 
-        for j in range(GATES):
-            load_scales(nc.gpsimd, F32, j, slice(SYNC_SCALE_GROUPS, GROUPS))
+        if SYNC_SCALE_GROUPS < GROUPS:
+            for j in range(GATES):
+                load_scales(nc.gpsimd, F32, j, slice(SYNC_SCALE_GROUPS, GROUPS))
 
         ident_bf16 = keep.tile([P, P], BF16)
         make_identity(nc, ident_bf16[:])

@@ -22,7 +22,7 @@ UNIT_K = UNIT_GROUPS * K_PASS
 UNITS = GROUPS // UNIT_GROUPS
 SLOTS = T * UNIT_GROUPS
 RECURRENT_AT = UNITS - 2
-SYNC_SCALE_GROUPS = 32
+SYNC_SCALE_GROUPS = 16
 
 FLOPS = 2 * B * T * I * GATES * H + 2 * B * H * GATES * H
 
@@ -60,21 +60,23 @@ def tile_naivelstm_pa_k_kernel(
         ident_f32 = keep.tile([P, P], F32)
         make_identity(nc, ident_f32[:])
 
-        w_planes = keep.tile([P, GROUPS, GATES * H], U8, align_bytes=64)
+        early_planes = keep.tile([P, SYNC_SCALE_GROUPS, GATES * H], U8, align_bytes=64)
+        late_planes = keep.tile([P, GROUPS - SYNC_SCALE_GROUPS, GATES * H], U8, align_bytes=64)
         for j in range(GATES):
-            nc.vector.memset(w_planes[:, :, j * H : (j + 1) * H].bitcast(I32), 0)
+            nc.vector.memset(late_planes[:, :, j * H : (j + 1) * H].bitcast(I32), 0)
+        for j in range(GATES):
+            nc.vector.memset(early_planes[:, :, j * H : (j + 1) * H].bitcast(I32), 0)
 
-        def load_scales(queue, view, j, groups):
+        def load_scales(queue, view, j, planes, groups):
             scale_rows = gate_scales[j].rearrange("g (q r) n -> r q g n", r=4)
             for r in range(4):
                 queue.dma_start(
-                    out=w_planes[r : P : 32, groups, j * H : (j + 1) * H].bitcast(view),
+                    out=planes[r : P : 32, :, j * H : (j + 1) * H].bitcast(view),
                     in_=scale_rows[r][:, groups, :].bitcast(view),
                 )
 
-        if SYNC_SCALE_GROUPS < GROUPS:
-            for j in range(GATES):
-                load_scales(nc.gpsimd, F32, j, slice(SYNC_SCALE_GROUPS, GROUPS))
+        for j in range(GATES):
+            load_scales(nc.gpsimd, F32, j, late_planes, slice(SYNC_SCALE_GROUPS, GROUPS))
 
         ident_bf16 = keep.tile([P, P], BF16)
         make_identity(nc, ident_bf16[:])
@@ -112,7 +114,7 @@ def tile_naivelstm_pa_k_kernel(
 
         x_tiles = [load_x(0), load_x(1)]
         for j in range(GATES):
-            load_scales(nc.sync, I32, j, slice(0, SYNC_SCALE_GROUPS))
+            load_scales(nc.sync, I32, j, early_planes, slice(0, SYNC_SCALE_GROUPS))
         for m in range(UNITS):
             load_weights(m)
             if m + 2 < UNITS:
@@ -161,7 +163,7 @@ def tile_naivelstm_pa_k_kernel(
                         lhsT=x_codes[m][:, t * UNIT_GROUPS + gl, :].bitcast(FP8X4),
                         lhsT_scale=x_planes[m][:, t * UNIT_GROUPS + gl, :],
                         rhs=w_codes[:, g, :].bitcast(FP8X4),
-                        rhs_scale=w_planes[:, g, :],
+                        rhs_scale=(early_planes[:, g, :] if g < SYNC_SCALE_GROUPS else late_planes[:, g - SYNC_SCALE_GROUPS, :]),
                         start=(g == 0),
                         stop=(g == GROUPS - 1),
                     )

@@ -22,6 +22,7 @@ UNIT_K = UNIT_GROUPS * K_PASS
 UNITS = GROUPS // UNIT_GROUPS
 SLOTS = T * UNIT_GROUPS
 RECURRENT_AT = UNITS - 2
+GPSIMD_UNITS = 2
 SYNC_SCALE_GROUPS = 16
 
 FLOPS = 2 * B * T * I * GATES * H + 2 * B * H * GATES * H
@@ -57,15 +58,21 @@ def tile_naivelstm_pa_k_kernel(
         nc.vector.memset(warm[:], 0.0)
         nc.scalar.activation(out=warm[:], in_=warm[:], func=ACT.Sigmoid)
 
+        def load_x(queue, n):
+            x_raw = x_pool.tile([P, T, UNIT_K], BF16, name="x_raw")
+            queue.dma_start(out=x_raw[:], in_=inputs[:, :, n * UNIT_K : (n + 1) * UNIT_K])
+            return x_raw
+
+        x_tiles = [load_x(nc.gpsimd, 0)]
         ident_f32 = keep.tile([P, P], F32)
         make_identity(nc, ident_f32[:])
+        for n in range(1, GPSIMD_UNITS):
+            x_tiles.append(load_x(nc.gpsimd, n))
 
         early_planes = keep.tile([P, SYNC_SCALE_GROUPS, GATES * H], U8, align_bytes=64)
         late_planes = keep.tile([P, GROUPS - SYNC_SCALE_GROUPS, GATES * H], U8, align_bytes=64)
-        for j in range(GATES):
-            nc.vector.memset(late_planes[:, :, j * H : (j + 1) * H].bitcast(I32), 0)
-        for j in range(GATES):
-            nc.vector.memset(early_planes[:, :, j * H : (j + 1) * H].bitcast(I32), 0)
+        nc.vector.memset(early_planes[:].rearrange("p g n -> p (g n)").bitcast(I32), 0)
+        nc.vector.memset(late_planes[:].rearrange("p g n -> p (g n)").bitcast(I32), 0)
 
         def load_scales(queue, view, j, planes, groups):
             scale_rows = gate_scales[j].rearrange("g (q r) n -> r q g n", r=4)
@@ -98,11 +105,6 @@ def tile_naivelstm_pa_k_kernel(
 
         w_codes = keep.tile([P, GROUPS, GATES * H], U32, align_bytes=64)
 
-        def load_x(n):
-            x_raw = x_pool.tile([P, T, UNIT_K], BF16, name="x_raw")
-            nc.sync.dma_start(out=x_raw[:], in_=inputs[:, :, n * UNIT_K : (n + 1) * UNIT_K])
-            return x_raw
-
         def load_weights(m):
             groups = slice(m * UNIT_GROUPS, (m + 1) * UNIT_GROUPS)
             for j in range(GATES):
@@ -112,13 +114,14 @@ def tile_naivelstm_pa_k_kernel(
                     in_=words[:, groups, :].bitcast(I32),
                 )
 
-        x_tiles = [load_x(0), load_x(1)]
-        for j in range(GATES):
+        for j in range(GATES - 1):
             load_scales(nc.sync, I32, j, early_planes, slice(0, SYNC_SCALE_GROUPS))
-        for m in range(UNITS):
+        load_weights(0)
+        load_scales(nc.sync, I32, GATES - 1, early_planes, slice(0, SYNC_SCALE_GROUPS))
+        for m in range(1, UNITS):
+            if GPSIMD_UNITS <= m + 1 < UNITS:
+                x_tiles.append(load_x(nc.sync, m + 1))
             load_weights(m)
-            if m + 2 < UNITS:
-                x_tiles.append(load_x(m + 2))
 
         acc = [acc_pool.tile([P, GATES * H], F32, name="acc%d" % t) for t in range(T)]
         x_sorted = {}

from contextlib import ExitStack

import concourse.mybir as mybir
from concourse.masks import make_identity

BF16 = mybir.dt.bfloat16
F32 = mybir.dt.float32
I32 = mybir.dt.int32
U32 = mybir.dt.uint32
U8 = mybir.dt.uint8
FP8X4 = mybir.dt.float8_e4m3fn_x4
ACT = mybir.ActivationFunctionType
ALU = mybir.AluOpType

P = 128
B, T, I, H = 128, 4, 16384, 128
GATES = 4
K_PASS = 512
GROUPS = I // K_PASS
UNIT_GROUPS = 2
UNIT_K = UNIT_GROUPS * K_PASS
UNITS = GROUPS // UNIT_GROUPS
SLOTS = T * UNIT_GROUPS
RECURRENT_AT = UNITS - 2
GPSIMD_UNITS = 2
SYNC_SCALE_GROUPS = 16

FLOPS = 2 * B * T * I * GATES * H + 2 * B * H * GATES * H


def tile_naivelstm_pa_k_kernel(
    tc,
    inputs, h0, c0,
    w_ii_words, w_ii_scales, b_ii, w_hi, b_hi,
    w_if__words, w_if__scales, b_if_, w_hf, b_hf,
    w_io_words, w_io_scales, b_io, w_ho, b_ho,
    w_ig_words, w_ig_scales, b_ig, w_hg, b_hg,
    out_0, out_1, out_2,
):
    nc = tc.nc
    gate_words = [w_ii_words, w_if__words, w_io_words, w_ig_words]
    gate_scales = [w_ii_scales, w_if__scales, w_io_scales, w_ig_scales]
    gate_bias_x = [b_ii, b_if_, b_io, b_ig]
    gate_bias_h = [b_hi, b_hf, b_ho, b_hg]
    gate_w_h = [w_hi, w_hf, w_ho, w_hg]

    with ExitStack() as ctx:
        keep = ctx.enter_context(tc.tile_pool(name="keep", bufs=1))
        x_pool = ctx.enter_context(tc.tile_pool(name="x_pool", bufs=6))
        stage = ctx.enter_context(tc.tile_pool(name="stage", bufs=2))
        coded = ctx.enter_context(tc.tile_pool(name="coded", bufs=3))
        work = ctx.enter_context(tc.tile_pool(name="work", bufs=T))
        acc_pool = ctx.enter_context(tc.psum_pool(name="acc_pool", bufs=1))
        xt_pool = ctx.enter_context(tc.psum_pool(name="xt_pool", bufs=4))
        ctx.enter_context(tc.manual_schedule())

        warm = keep.tile([P, 1], F32)
        nc.vector.memset(warm[:], 0.0)
        nc.scalar.activation(out=warm[:], in_=warm[:], func=ACT.Sigmoid)

        def load_x(queue, n):
            x_raw = x_pool.tile([P, T, UNIT_K], BF16, name="x_raw")
            queue.dma_start(out=x_raw[:], in_=inputs[:, :, n * UNIT_K : (n + 1) * UNIT_K])
            return x_raw

        x_tiles = [load_x(nc.gpsimd, 0)]
        ident_f32 = keep.tile([P, P], F32)
        make_identity(nc, ident_f32[:])
        for n in range(1, GPSIMD_UNITS):
            x_tiles.append(load_x(nc.gpsimd, n))

        early_planes = keep.tile([P, SYNC_SCALE_GROUPS, GATES * H], U8, align_bytes=64)
        late_planes = keep.tile([P, GROUPS - SYNC_SCALE_GROUPS, GATES * H], U8, align_bytes=64)
        nc.vector.memset(early_planes[:].rearrange("p g n -> p (g n)").bitcast(I32), 0)
        nc.vector.memset(late_planes[:].rearrange("p g n -> p (g n)").bitcast(I32), 0)

        def load_scales(queue, view, j, planes, groups):
            scale_rows = gate_scales[j].rearrange("g (q r) n -> r q g n", r=4)
            for r in range(4):
                queue.dma_start(
                    out=planes[r : P : 32, :, j * H : (j + 1) * H].bitcast(view),
                    in_=scale_rows[r][:, groups, :].bitcast(view),
                )

        for j in range(GATES):
            load_scales(nc.gpsimd, F32, j, late_planes, slice(SYNC_SCALE_GROUPS, GROUPS))

        ident_bf16 = keep.tile([P, P], BF16)
        make_identity(nc, ident_bf16[:])
        ones = keep.tile([P, P], BF16)
        nc.vector.memset(ones[:], 1.0)
        bias_rows = keep.tile([P, GATES * H], BF16)
        nc.vector.memset(bias_rows[:], 0.0)

        rec_rows = keep.tile([P, 1 + GATES, H], BF16)
        nc.gpsimd.dma_start(out=rec_rows[:, 0, :], in_=h0[0])
        for j in range(GATES):
            nc.gpsimd.dma_start(out=rec_rows[:, 1 + j, :], in_=gate_w_h[j])
        for j in range(GATES):
            cols = slice(j * H, (j + 1) * H)
            nc.gpsimd.dma_start(out=bias_rows[0:1, cols], in_=gate_bias_x[j].rearrange("h o -> o h"))
            nc.gpsimd.dma_start(out=bias_rows[1:2, cols], in_=gate_bias_h[j].rearrange("h o -> o h"))
        c0_sb = keep.tile([P, H], BF16)
        nc.gpsimd.dma_start(out=c0_sb[:], in_=c0[0])

        w_codes = keep.tile([P, GROUPS, GATES * H], U32, align_bytes=64)

        def load_weights(m):
            groups = slice(m * UNIT_GROUPS, (m + 1) * UNIT_GROUPS)
            for j in range(GATES):
                words = gate_words[j].rearrange("g p n t -> p g (n t)")
                nc.sync.dma_start(
                    out=w_codes[:, groups, j * H : (j + 1) * H].bitcast(I32),
                    in_=words[:, groups, :].bitcast(I32),
                )

        for j in range(GATES - 1):
            load_scales(nc.sync, I32, j, early_planes, slice(0, SYNC_SCALE_GROUPS))
        load_weights(0)
        load_scales(nc.sync, I32, GATES - 1, early_planes, slice(0, SYNC_SCALE_GROUPS))
        for m in range(1, UNITS):
            if GPSIMD_UNITS <= m + 1 < UNITS:
                x_tiles.append(load_x(nc.sync, m + 1))
            load_weights(m)

        acc = [acc_pool.tile([P, GATES * H], F32, name="acc%d" % t) for t in range(T)]
        x_sorted = {}
        x_grouped = {}
        x_codes = {}
        x_planes = {}

        def sort_x(n):
            x_sorted[n] = stage.tile([P, SLOTS, 2, P], F32, name="x_sorted")
            nc.vector.tensor_copy(
                out=x_sorted[n][:],
                in_=x_tiles[n][:].rearrange("b t k -> b (t k)").bitcast(F32).rearrange("b (s p u) -> b s u p", p=P, u=2),
            )

        def transpose_x(n):
            x_grouped[n] = stage.tile([P, SLOTS, B, 4], BF16, name="x_grouped", align_bytes=64)
            for first in range(0, SLOTS, 2):
                xt = xt_pool.tile([P, 2, 2, B], F32, name="xt")
                for gl in range(2):
                    for u in range(2):
                        nc.tensor.transpose(xt[:, gl, u, :], x_sorted[n][:, first + gl, u, :], ident_f32[:])
                nc.scalar.copy(
                    out=x_grouped[n][:, first : first + 2].bitcast(F32),
                    in_=xt[:].rearrange("p g u b -> p g b u"),
                )

        def quantise_x(n):
            x_codes[n] = coded.tile([P, SLOTS, B], U32, name="x_codes", align_bytes=64)
            x_planes[n] = coded.tile([P, SLOTS, B], U8, name="x_planes", align_bytes=64)
            nc.vector.quantize_mx(
                out=x_codes[n][:].rearrange("p s b -> p (s b)").bitcast(FP8X4),
                scales=x_planes[n][:].rearrange("p s b -> p (s b)"),
                in_=x_grouped[n][:].rearrange("p s b j -> p (s b j)"),
            )

        def multiply_run(m):
            for t in range(T):
                for gl in range(UNIT_GROUPS):
                    g = m * UNIT_GROUPS + gl
                    nc.tensor.matmul_mx(
                        out=acc[t][:],
                        lhsT=x_codes[m][:, t * UNIT_GROUPS + gl, :].bitcast(FP8X4),
                        lhsT_scale=x_planes[m][:, t * UNIT_GROUPS + gl, :],
                        rhs=w_codes[:, g, :].bitcast(FP8X4),
                        rhs_scale=(early_planes[:, g, :] if g < SYNC_SCALE_GROUPS else late_planes[:, g - SYNC_SCALE_GROUPS, :]),
                        start=(g == 0),
                        stop=(g == GROUPS - 1),
                    )

        rec_cols = keep.tile([P, 1 + GATES, H], BF16)
        hidden = keep.tile([P, GATES * H], F32)

        def transpose_recurrent():
            rec_ps = xt_pool.tile([P, 1 + GATES, H], BF16, name="rec_ps", tag="xt")
            for j in range(1 + GATES):
                nc.tensor.transpose(rec_ps[:, j, :], rec_rows[:, j, :], ident_bf16[:])
            nc.scalar.copy(out=rec_cols[:], in_=rec_ps[:])

        def multiply_recurrent():
            hid_ps = xt_pool.tile([P, GATES * H], F32, name="hid_ps", tag="xt")
            nc.tensor.matmul(
                out=hid_ps[:],
                lhsT=rec_cols[:, 0, :],
                rhs=rec_cols[:, 1:, :].rearrange("p j n -> p (j n)"),
                start=True,
                stop=False,
            )
            nc.tensor.matmul(out=hid_ps[:], lhsT=ones[:], rhs=bias_rows[:], start=False, stop=True)
            nc.scalar.copy(out=hidden[:], in_=hid_ps[:])

        sort_x(0)
        transpose_x(0)
        for n in range(UNITS):
            if n + 1 < UNITS:
                sort_x(n + 1)
            quantise_x(n)
            if n + 1 < UNITS:
                transpose_x(n + 1)
            if n == RECURRENT_AT:
                transpose_recurrent()
            multiply_run(n)
            if n == RECURRENT_AT:
                multiply_recurrent()

        gates = []
        for t in range(T):
            z = work.tile([P, GATES * H], F32, name="z")
            nc.vector.tensor_tensor(out=z[:], in0=acc[t][:], in1=hidden[:], op=ALU.add)
            gate = work.tile([P, GATES, H], F32, name="gate")
            flat = gate[:].rearrange("p j n -> p (j n)")
            nc.scalar.activation(out=flat[:, 0 : 3 * H], in_=z[:, 0 : 3 * H], func=ACT.Sigmoid)
            nc.scalar.activation(out=flat[:, 3 * H :], in_=z[:, 3 * H :], func=ACT.Tanh)
            gates.append(gate)
        cells = []
        for t in range(T):
            gate = gates[t]
            kept = work.tile([P, H], F32, name="kept")
            nc.vector.tensor_tensor(out=kept[:], in0=gate[:, 1, :], in1=c0_sb[:], op=ALU.mult)
            fresh = work.tile([P, H], F32, name="fresh")
            nc.vector.tensor_tensor(out=fresh[:], in0=gate[:, 0, :], in1=gate[:, 3, :], op=ALU.mult)
            c_next = work.tile([P, H], F32, name="c_next")
            nc.vector.tensor_tensor(out=c_next[:], in0=kept[:], in1=fresh[:], op=ALU.add)
            tanh_c = work.tile([P, H], F32, name="tanh_c")
            nc.scalar.activation(out=tanh_c[:], in_=c_next[:], func=ACT.Tanh)
            cells.append((c_next, tanh_c))
        nc.sync.dma_start(out=out_2[0], in_=cells[T - 1][0][:])
        for t in range(T):
            h_next = work.tile([P, H], F32, name="h_next")
            nc.vector.tensor_tensor(out=h_next[:], in0=gates[t][:, 2, :], in1=cells[t][1][:], op=ALU.mult)
            nc.sync.dma_start(out=out_0[t], in_=h_next[:])
            if t == T - 1:
                nc.sync.dma_start(out=out_1[0], in_=h_next[:])
